import numpy as np
import ml_dtypes


def mxq(x, axis, fmt="e4m3"):
    dtype, down = {"e4m3": (ml_dtypes.float8_e4m3fn, 7), "e5m2": (ml_dtypes.float8_e5m2, 14)}[fmt]
    v = np.moveaxis(np.asarray(x, np.float32).astype(ml_dtypes.bfloat16).astype(np.float64), axis, -1)
    blocks = v.reshape(v.shape[:-1] + (-1, 32))
    amax = np.abs(blocks).max(-1, keepdims=True)
    byte = np.maximum(np.where(amax > 0, np.frexp(amax)[1] - 1 + 127, 0) - down, 1)
    scale = np.exp2(byte - 127.0)
    codes = (blocks / scale).astype(np.float32).astype(dtype).astype(np.float64)
    return np.moveaxis((codes * scale).reshape(v.shape), -1, axis)


WIDE = False


def mx_kscale(k):
    if not WIDE:
        return np.ones(k)
    levels = np.array([10, -10, 5, -5, 0])
    if k % 512:
        return np.exp2(np.random.permutation(np.resize(levels, k // 32))).repeat(32)
    a = np.empty((k // 512, 16))
    for p in range(k // 512):
        a[p, :8] = np.random.permutation(np.resize(levels, 8))
        for g in range(8):
            far = levels[np.abs(levels - a[p, g]) >= 10]
            a[p, g + 8] = far[np.random.randint(len(far))]
    return np.exp2(a.ravel()).repeat(32)


BF16 = ml_dtypes.bfloat16


def bf(x):
    return np.asarray(x, np.float32).astype(BF16)


def f64(x):
    return np.asarray(x).astype(np.float64)


B, HI, WI, F, D, NH, C = 1, 32, 32, 1024, 256, 3, 16
N = HI * WI
EPS = 1e-12


def l2norm_rows(a):
    n = np.sqrt(np.sum(a * a, axis=1, keepdims=True))
    return a / np.maximum(n, EPS)


def setup_inputs():
    s = mx_kscale(F)

    def w():
        return bf(np.random.standard_normal((D, F)) / np.sqrt(F) / s[None, :])

    def b():
        return bf(np.random.standard_normal(D) * 0.2)

    return {"x": bf(np.random.standard_normal((B, F, HI, WI)) * s[None, :, None, None]),
            "W1": w(), "b1": b(), "W2": w(), "b2": b(), "W3": w(), "b3": b()}


def core(x, W1, b1, W2, b2, W3, b3):
    xq = mxq(f64(x).reshape(F, N).T, 1, "e4m3")
    heads = [l2norm_rows((xq @ mxq(f64(W), 1, "e4m3").T) + f64(b)) for W, b in ((W1, b1), (W2, b2), (W3, b3))]
    return np.stack(heads)


def e4m3fn_bytes(y):
    return np.clip(np.asarray(y, np.float64), -448.0, 448.0).astype(np.float32).astype(ml_dtypes.float8_e4m3fn).view(np.uint8)


def reference(x, W1, b1, W2, b2, W3, b3):
    out = core(x, W1, b1, W2, b2, W3, b3)
    s = np.max(np.abs(out), axis=-1, keepdims=True) / 448.0
    return out, e4m3fn_bytes(out / s)

@@ -1,0 +1,415 @@
+from contextlib import ExitStack
+
+import concourse.mybir as mybir
+from concourse.masks import make_identity
+
+F32 = mybir.dt.float32
+BF16 = mybir.dt.bfloat16
+U32 = mybir.dt.uint32
+U8 = mybir.dt.uint8
+FP8X4 = mybir.dt.float8_e4m3fn_x4
+FP8 = mybir.dt.float8_e4m3fn
+ALU = mybir.AluOpType
+ACT = mybir.ActivationFunctionType
+AX = mybir.AxisListType
+
+P = 128
+FEAT = 1024
+NODES = 1024
+D = 256
+HEADS = 3
+FLOPS = 2 * NODES * FEAT * D * HEADS
+
+
+def tile_gat_pa_kernel(tc, x, W1, b1, W2, b2, W3, b3, out_0, out_1):
+    nc = tc.nc
+    weights = (W1, W2, W3)
+    biases = (b1, b2, b3)
+    xf = x.rearrange("b f h w -> (b f) (h w)")
+
+    with ExitStack() as ctx:
+        keep = ctx.enter_context(tc.tile_pool(name="keep", bufs=1))
+        junk = ctx.enter_context(tc.tile_pool(name="junk", bufs=2))
+        ps_t = ctx.enter_context(tc.psum_pool(name="ps_t", bufs=2))
+        ps_a = ctx.enter_context(tc.psum_pool(name="ps_a", bufs=6))
+        ctx.enter_context(tc.manual_schedule())
+
+        brow = keep.tile([P, HEADS * D], BF16, name="brow")
+        ones = keep.tile([P, P], BF16, name="ones")
+        warm = keep.tile([P, 1], F32, name="warm")
+        warm2 = keep.tile([P, 1], F32, name="warm2")
+        zero = keep.tile([P, 1], F32, name="zero")
+        ident = keep.tile([P, P], F32, name="ident")
+        identb = keep.tile([P, P], BF16, name="identb")
+        bias = keep.tile([P, HEADS * D], F32, name="bias")
+        wraw = [keep.tile([P, 2, FEAT], BF16, name="wraw%d" % k) for k in range(HEADS)]
+        xraw = {}
+        wg = {}
+        wc = {}
+        ws = {}
+        xg = {}
+        xc = {}
+        xs = {}
+        for g in range(2):
+            for c in range(2):
+                xraw[(g, c)] = keep.tile([P, 4, 512], BF16, name="xraw%d%d" % (g, c))
+            for k in range(HEADS):
+                wg[(k, g)] = keep.tile([P, 4 * D], BF16, name="wg%d%d" % (k, g), align_bytes=64)
+                wc[(k, g)] = keep.tile([P, D], U32, name="wc%d%d" % (k, g), align_bytes=64)
+                ws[(k, g)] = keep.tile([P, D], U8, name="ws%d%d" % (k, g), align_bytes=64)
+            for j in range(4):
+                xg[(g, j)] = keep.tile([P, 256, 4], BF16, name="xg%d%d" % (g, j), align_bytes=64)
+                xc[(g, j)] = keep.tile([P, 256], U32, name="xc%d%d" % (g, j), align_bytes=64)
+                xs[(g, j)] = keep.tile([P, 256], U8, name="xs%d%d" % (g, j), align_bytes=64)
+        h = {}
+        ss = {}
+        st = {}
+        rc = {}
+        sc = {}
+        o0 = {}
+        o1 = {}
+        for k in range(HEADS):
+            for c in range(2):
+                h[(k, c)] = keep.tile([P, 4, D], F32, name="h%d%d" % (k, c))
+                ss[(k, c)] = keep.tile([P, 4], F32, name="ss%d%d" % (k, c))
+                st[(k, c)] = keep.tile([P, 2, 4], F32, name="st%d%d" % (k, c))
+                rc[(k, c)] = keep.tile([P, 2, 4], F32, name="rc%d%d" % (k, c))
+                sc[(k, c)] = keep.tile([P, 2, 4], F32, name="sc%d%d" % (k, c))
+            for j in range(4):
+                o0[(k, j)] = keep.tile([P, 2, D], F32, name="o0%d%d" % (k, j))
+                o1[(k, j)] = keep.tile([P, 2, D], FP8, name="o1%d%d" % (k, j))
+        tps = {}
+        accs = {}
+
+        def load_w(k):
+            nc.sync.dma_start(out=wraw[k][:], in_=weights[k].rearrange("(a p) f -> p a f", p=P))
+
+        def load_bias():
+            for k in range(HEADS):
+                nc.sync.dma_start(out=brow[0:1, D * k : D * (k + 1)], in_=biases[k].rearrange("(o d) -> o d", o=1))
+
+        def load_x(g, c):
+            nc.sync.dma_start(
+                out=xraw[(g, c)][:],
+                in_=xf[512 * g : 512 * (g + 1), 512 * c : 512 * (c + 1)].rearrange("(p j) w -> p j w", j=4),
+            )
+
+        def bias_matmul():
+            pb0 = ps_a.tile([P, 512], F32, tag="acc")
+            nc.tensor.matmul(out=pb0[:], lhsT=ones[:], rhs=brow[:, 0:512], start=True, stop=True)
+            pb1 = ps_a.tile([P, 512], F32, tag="acc")
+            nc.tensor.matmul(out=pb1[:, 0:256], lhsT=ones[:], rhs=brow[:, 512:768], start=True, stop=True)
+            accs["b0"] = pb0
+            accs["b1"] = pb1
+
+        def bias_copy():
+            nc.scalar.copy(out=bias[:, 0:512], in_=accs["b0"][:])
+            nc.scalar.copy(out=bias[:, 512:768], in_=accs["b1"][:, 0:256])
+
+        def transposes(k, g):
+            tp = ps_t.tile([P, 4, P], F32, tag="tp")
+            for a in range(2):
+                words = wraw[k][:, a, :].bitcast(F32)
+                for u in range(2):
+                    nc.tensor.transpose(tp[:, 2 * a + u, :], words[:, 256 * g + u : 256 * (g + 1) : 2], ident[:])
+            tps[(k, g)] = tp
+
+        def w_copy(k, g):
+            nc.scalar.copy(
+                out=wg[(k, g)][:].bitcast(F32).rearrange("p (a r u) -> p a r u", a=2, u=2),
+                in_=tps[(k, g)][:].rearrange("p (a u) r -> p a r u", u=2),
+            )
+
+        def w_quant(k, g):
+            nc.vector.quantize_mx(out=wc[(k, g)][:].bitcast(FP8X4), scales=ws[(k, g)][:], in_=wg[(k, g)][:])
+
+        def x_interleave(g, j, eng):
+            src = xraw[(g, j // 2)][:, :, 256 * (j % 2) : 256 * (j % 2) + 256].rearrange("q j w -> q w j")
+            dst = xg[(g, j)][:]
+            if eng == "v":
+                nc.vector.tensor_copy(out=dst, in_=src)
+            else:
+                nc.scalar.copy(out=dst, in_=src)
+
+        def pe_interleave(g, j):
+            pil = ps_a.tile([P, 1024], BF16, tag="acc")
+            for u in range(2):
+                nc.tensor.matmul(
+                    out=pil[:].rearrange("q (t p u e) -> q u t p e", t=2, u=2, e=2)[:, u],
+                    lhsT=identb[:],
+                    rhs=xraw[(g, j // 2)][:, 2 * u : 2 * u + 2, 256 * (j % 2) : 256 * (j % 2) + 256].rearrange(
+                        "q e (p t) -> q t p e", t=2
+                    ),
+                    start=True,
+                    stop=True,
+                )
+            accs[("x", g, j)] = pil
+
+        def x_copy(g, j):
+            nc.scalar.copy(out=xg[(g, j)][:].rearrange("q w j -> q (w j)"), in_=accs[("x", g, j)][:])
+
+        def x_quant(g, j):
+            nc.vector.quantize_mx(
+                out=xc[(g, j)][:].bitcast(FP8X4), scales=xs[(g, j)][:], in_=xg[(g, j)][:].rearrange("p w j -> p (w j)")
+            )
+
+        def mm(k, j):
+            acc = ps_a.tile([P, 2, D], F32, tag="acc")
+            for t in range(2):
+                for g in range(2):
+                    nc.tensor.matmul_mx(
+                        out=acc[:, t, :],
+                        lhsT=xc[(g, j)][:, P * t : P * (t + 1)].bitcast(FP8X4),
+                        lhsT_scale=xs[(g, j)][:, P * t : P * (t + 1)],
+                        rhs=wc[(k, g)][:].bitcast(FP8X4),
+                        rhs_scale=ws[(k, g)][:],
+                        start=(g == 0),
+                        stop=(g == 1),
+                    )
+            accs[(k, j)] = acc
+
+        def rows(j):
+            return 2 * (j % 2)
+
+        def add_bias(k, j):
+            r = rows(j)
+            nc.vector.tensor_tensor(
+                out=h[(k, j // 2)][:, r : r + 2, :],
+                in0=accs[(k, j)][:],
+                in1=bias[:, D * k : D * (k + 1)].unsqueeze(1).to_broadcast([P, 2, D]),
+                op=ALU.add,
+            )
+
+        def sumsq(k, j):
+            for t in range(2):
+                r = rows(j) + t
+                sq = junk.tile([P, D], BF16, tag="sq")
+                nc.scalar.activation(
+                    out=sq[:], in_=h[(k, j // 2)][:, r, :], func=ACT.Square, accum_out=ss[(k, j // 2)][:, r : r + 1]
+                )
+
+        def absmax(k, c, r0, n):
+            nc.vector.tensor_reduce(
+                out=st[(k, c)][:, 1, r0 : r0 + n],
+                in_=h[(k, c)][:, r0 : r0 + n, :],
+                axis=AX.X,
+                op=ALU.max,
+                apply_absolute_value=True,
+            )
+
+        def clamp(k, c, r0, n):
+            nc.vector.tensor_scalar(
+                out=st[(k, c)][:, 0, r0 : r0 + n], in0=ss[(k, c)][:, r0 : r0 + n], scalar1=1e-24, scalar2=None, op0=ALU.max
+            )
+
+        def recip(k, c, r0, n):
+            nc.vector.reciprocal(out=rc[(k, c)][:, :, r0 : r0 + n], in_=st[(k, c)][:, :, r0 : r0 + n])
+
+        def factors(k, c, r0, n):
+            nc.scalar.activation(out=sc[(k, c)][:, 0, r0 : r0 + n], in_=rc[(k, c)][:, 0, r0 : r0 + n], func=ACT.Sqrt)
+            nc.scalar.activation(
+                out=sc[(k, c)][:, 1, r0 : r0 + n], in_=rc[(k, c)][:, 1, r0 : r0 + n], func=ACT.Copy, scale=448.0
+            )
+
+        def scale_row(k, j, t, eng):
+            r = rows(j) + t
+            if eng == "v":
+                nc.vector.tensor_scalar(
+                    out=o0[(k, j)][:, t, :],
+                    in0=h[(k, j // 2)][:, r, :],
+                    scalar1=sc[(k, j // 2)][:, 0, r : r + 1],
+                    scalar2=None,
+                    op0=ALU.mult,
+                )
+            elif eng == "g":
+                nc.gpsimd.tensor_scalar(
+                    out=o0[(k, j)][:, t, :],
+                    in0=h[(k, j // 2)][:, r, :],
+                    scalar1=sc[(k, j // 2)][:, 0, r : r + 1],
+                    scalar2=0.0,
+                    op0=ALU.mult,
+                    op1=ALU.add,
+                )
+            else:
+                nc.scalar.activation(
+                    out=o0[(k, j)][:, t, :], in_=h[(k, j // 2)][:, r, :], func=ACT.Copy, scale=sc[(k, j // 2)][:, 0, r : r + 1]
+                )
+
+        def cast_row(k, j, t, eng):
+            r = rows(j) + t
+            if eng == "v":
+                nc.vector.tensor_scalar(
+                    out=o1[(k, j)][:, t, :],
+                    in0=h[(k, j // 2)][:, r, :],
+                    scalar1=sc[(k, j // 2)][:, 1, r : r + 1],
+                    scalar2=None,
+                    op0=ALU.mult,
+                    saturate=False,
+                )
+            else:
+                nc.scalar.activation(
+                    out=o1[(k, j)][:, t, :],
+                    in_=h[(k, j // 2)][:, r, :],
+                    func=ACT.Identity,
+                    scale=sc[(k, j // 2)][:, 1, r : r + 1],
+                    bias=zero[:, 0:1],
+                    saturate=False,
+                )
+
+        def node_view(ap, k, j):
+            rows_of_unit = ap[k, 256 * j : 256 * (j + 1), :]
+            if j % 2 == 0:
+                return rows_of_unit.rearrange("(t p) d -> p t d", t=2)
+            return rows_of_unit.rearrange("(p t) d -> p t d", t=2)
+
+        def store0(k, j):
+            nc.sync.dma_start(out=node_view(out_0, k, j), in_=o0[(k, j)][:])
+
+        def store1(k, j):
+            nc.sync.dma_start(out=node_view(out_1, k, j), in_=o1[(k, j)][:].bitcast(U8))
+
+        def finish_first(u, eng):
+            scale_row(u[0], u[1], 0, eng)
+            scale_row(u[0], u[1], 1, eng)
+            store0(u[0], u[1])
+            cast_row(u[0], u[1], 0, "s")
+            cast_row(u[0], u[1], 1, "s")
+            store1(u[0], u[1])
+
+        def finish_second(u, eng):
+            scale_row(u[0], u[1], 0, eng)
+            scale_row(u[0], u[1], 1, eng)
+            store0(u[0], u[1])
+            cast_row(u[0], u[1], 0, "s")
+            cast_row(u[0], u[1], 1, "s")
+            store1(u[0], u[1])
+
+        nc.vector.memset(brow[:], 0.0)
+        nc.vector.memset(warm[:], 1.0)
+        nc.vector.memset(ones[:], 1.0)
+        nc.vector.memset(zero[:], 0.0)
+        nc.scalar.activation(out=warm2[:], in_=warm[:], func=ACT.Sqrt)
+        make_identity(nc, ident[:])
+        make_identity(nc, identb[:])
+
+        load_w(0)
+        load_bias()
+        load_x(0, 0)
+        load_x(1, 0)
+        load_x(0, 1)
+        load_x(1, 1)
+        load_w(1)
+        load_w(2)
+
+        transposes(0, 0)
+        transposes(0, 1)
+        bias_matmul()
+        pe_interleave(0, 1)
+        w_copy(0, 0)
+        x_interleave(0, 0, "v")
+        w_quant(0, 0)
+        x_quant(0, 0)
+        w_copy(0, 1)
+        bias_copy()
+        x_copy(0, 1)
+        pe_interleave(1, 1)
+        x_interleave(1, 0, "v")
+        w_quant(0, 1)
+        x_quant(1, 0)
+        x_copy(1, 1)
+        x_interleave(0, 2, "v")
+        x_quant(0, 1)
+        mm(0, 0)
+        pe_interleave(0, 3)
+        x_copy(0, 3)
+        x_quant(0, 2)
+        x_quant(1, 1)
+        mm(0, 1)
+        x_interleave(1, 2, "v")
+        pe_interleave(1, 3)
+
+        units = [(k, j) for k in range(HEADS) for j in range(4)]
+
+        add_bias(0, 0)
+        x_quant(1, 2)
+        sumsq(0, 0)
+        add_bias(0, 1)
+        x_copy(1, 3)
+        sumsq(0, 1)
+        x_quant(0, 3)
+        absmax(0, 0, 0, 4)
+        x_quant(1, 3)
+        transposes(1, 0)
+        transposes(1, 1)
+        mm(0, 2)
+        mm(0, 3)
+        clamp(0, 0, 0, 4)
+        w_copy(1, 0)
+        w_copy(1, 1)
+        add_bias(0, 2)
+        sumsq(0, 2)
+        recip(0, 0, 0, 4)
+        factors(0, 0, 0, 4)
+        w_quant(1, 0)
+        transposes(2, 0)
+        transposes(2, 1)
+        w_copy(2, 0)
+        w_copy(2, 1)
+        add_bias(0, 3)
+        sumsq(0, 3)
+        w_quant(1, 1)
+        finish_first(units[0], "g")
+        absmax(0, 1, 0, 4)
+        w_quant(2, 0)
+        w_quant(2, 1)
+        mm(1, 0)
+        mm(1, 1)
+        clamp(0, 1, 0, 4)
+        finish_second(units[1], "v")
+        recip(0, 1, 0, 4)
+        factors(0, 1, 0, 4)
+
+        for i in range(2, 5):
+            u0 = units[2 * i]
+            u1 = units[2 * i + 1]
+            k = u0[0]
+            c = u0[1] // 2
+            add_bias(u0[0], u0[1])
+            sumsq(u0[0], u0[1])
+            add_bias(u1[0], u1[1])
+            sumsq(u1[0], u1[1])
+            finish_first(units[2 * i - 2], "g")
+            absmax(k, c, 0, 4)
+            mm(units[2 * i + 2][0], units[2 * i + 2][1])
+            mm(units[2 * i + 3][0], units[2 * i + 3][1])
+            clamp(k, c, 0, 4)
+            finish_second(units[2 * i - 1], "v")
+            recip(k, c, 0, 4)
+            factors(k, c, 0, 4)
+
+        add_bias(2, 2)
+        sumsq(2, 2)
+        add_bias(2, 3)
+        sumsq(2, 3)
+        absmax(2, 1, 0, 2)
+        finish_first(units[8], "g")
+        clamp(2, 1, 0, 2)
+        absmax(2, 1, 2, 2)
+        recip(2, 1, 0, 2)
+        factors(2, 1, 0, 2)
+        finish_second(units[9], "v")
+        clamp(2, 1, 2, 2)
+        scale_row(2, 2, 0, "v")
+        recip(2, 1, 2, 2)
+        scale_row(2, 2, 1, "v")
+        store0(2, 2)
+        factors(2, 1, 2, 2)
+        cast_row(2, 2, 0, "s")
+        cast_row(2, 2, 1, "s")
+        store1(2, 2)
+        scale_row(2, 3, 0, "v")
+        scale_row(2, 3, 1, "v")
+        store0(2, 3)
+        cast_row(2, 3, 0, "s")
+        cast_row(2, 3, 1, "v")
+        store1(2, 3)

@@ -337,7 +337,8 @@ def tile_gat_pa_kernel(tc, x, W1, b1, W2, b2, W3, b3, out_0, out_1):
         x_copy(1, 3)
         sumsq(0, 1)
         x_quant(0, 3)
-        absmax(0, 0, 0, 4)
+        absmax(0, 0, 0, 2)
+        absmax(0, 0, 2, 2)
         x_quant(1, 3)
         transposes(1, 0)
         transposes(1, 1)
@@ -359,7 +360,8 @@ def tile_gat_pa_kernel(tc, x, W1, b1, W2, b2, W3, b3, out_0, out_1):
         sumsq(0, 3)
         w_quant(1, 1)
         finish_first(units[0], "g")
-        absmax(0, 1, 0, 4)
+        absmax(0, 1, 0, 2)
+        absmax(0, 1, 2, 2)
         w_quant(2, 0)
         w_quant(2, 1)
         mm(1, 0)
@@ -379,7 +381,8 @@ def tile_gat_pa_kernel(tc, x, W1, b1, W2, b2, W3, b3, out_0, out_1):
             add_bias(u1[0], u1[1])
             sumsq(u1[0], u1[1])
             finish_first(units[2 * i - 2], "g")
-            absmax(k, c, 0, 4)
+            absmax(k, c, 0, 2)
+            absmax(k, c, 2, 2)
             mm(units[2 * i + 2][0], units[2 * i + 2][1])
             mm(units[2 * i + 3][0], units[2 * i + 3][1])
             clamp(k, c, 0, 4)

@@ -366,53 +366,66 @@ def tile_gat_pa_kernel(tc, x, W1, b1, W2, b2, W3, b3, out_0, out_1):
         w_quant(2, 1)
         mm(1, 0)
         mm(1, 1)
+
+        def scale_unit(u, eng):
+            scale_row(u[0], u[1], 0, eng)
+            scale_row(u[0], u[1], 1, eng)
+            store0(u[0], u[1])
+
+        def cast_unit(u):
+            cast_row(u[0], u[1], 0, "s")
+            cast_row(u[0], u[1], 1, "s")
+            store1(u[0], u[1])
+
+        add_bias(1, 0)
         clamp(0, 1, 0, 4)
-        finish_second(units[1], "v")
+        scale_unit(units[1], "v")
+        cast_unit(units[1])
+        sumsq(1, 0)
         recip(0, 1, 0, 4)
         factors(0, 1, 0, 4)
 
         for i in range(2, 5):
-            u0 = units[2 * i]
             u1 = units[2 * i + 1]
-            k = u0[0]
-            c = u0[1] // 2
-            add_bias(u0[0], u0[1])
-            sumsq(u0[0], u0[1])
+            k = u1[0]
+            c = u1[1] // 2
             add_bias(u1[0], u1[1])
             sumsq(u1[0], u1[1])
-            finish_first(units[2 * i - 2], "g")
+            scale_unit(units[2 * i - 2], "g")
+            cast_unit(units[2 * i - 2])
+            cast_unit(units[2 * i - 1])
             absmax(k, c, 0, 2)
             absmax(k, c, 2, 2)
             mm(units[2 * i + 2][0], units[2 * i + 2][1])
             mm(units[2 * i + 3][0], units[2 * i + 3][1])
+            add_bias(units[2 * i + 2][0], units[2 * i + 2][1])
+            sumsq(units[2 * i + 2][0], units[2 * i + 2][1])
             clamp(k, c, 0, 4)
-            finish_second(units[2 * i - 1], "v")
+            scale_unit(units[2 * i - 1], "v")
             recip(k, c, 0, 4)
             factors(k, c, 0, 4)
 
-        add_bias(2, 2)
-        sumsq(2, 2)
         add_bias(2, 3)
         sumsq(2, 3)
         absmax(2, 1, 0, 2)
-        finish_first(units[8], "g")
+        scale_unit(units[8], "v")
+        cast_unit(units[8])
         clamp(2, 1, 0, 2)
         absmax(2, 1, 2, 2)
         recip(2, 1, 0, 2)
         factors(2, 1, 0, 2)
-        finish_second(units[9], "v")
+        scale_unit(units[9], "v")
         clamp(2, 1, 2, 2)
-        scale_row(2, 2, 0, "v")
+        cast_row(2, 1, 0, "v")
+        cast_row(2, 1, 1, "v")
+        store1(2, 1)
         recip(2, 1, 2, 2)
-        scale_row(2, 2, 1, "v")
-        store0(2, 2)
         factors(2, 1, 2, 2)
+        scale_unit(units[10], "v")
         cast_row(2, 2, 0, "s")
-        cast_row(2, 2, 1, "s")
+        cast_row(2, 2, 1, "v")
         store1(2, 2)
-        scale_row(2, 3, 0, "v")
-        scale_row(2, 3, 1, "v")
-        store0(2, 3)
+        scale_unit(units[11], "v")
         cast_row(2, 3, 0, "s")
         cast_row(2, 3, 1, "v")
         store1(2, 3)

@@ -124,8 +124,8 @@ def tile_gat_pa_kernel(tc, x, W1, b1, W2, b2, W3, b3, out_0, out_1):
             nc.vector.quantize_mx(out=wc[(k, g)][:].bitcast(FP8X4), scales=ws[(k, g)][:], in_=wg[(k, g)][:])
 
         def x_interleave(g, j, eng):
-            src = xraw[(g, j // 2)][:, :, 256 * (j % 2) : 256 * (j % 2) + 256].rearrange("q j w -> q w j")
-            dst = xg[(g, j)][:]
+            src = xraw[(g, j // 2)][:, :, 256 * (j % 2) : 256 * (j % 2) + 256].rearrange("q j (c i) -> q c j i", i=4)
+            dst = xg[(g, j)][:].rearrange("q (c i) j -> q c j i", i=4)
             if eng == "v":
                 nc.vector.tensor_copy(out=dst, in_=src)
             else:

@@ -71,10 +71,10 @@ def tile_gat_pa_kernel(tc, x, W1, b1, W2, b2, W3, b3, out_0, out_1):
         for k in range(HEADS):
             for c in range(2):
                 h[(k, c)] = keep.tile([P, 4, D], F32, name="h%d%d" % (k, c))
-                ss[(k, c)] = keep.tile([P, 4], F32, name="ss%d%d" % (k, c))
+                ss[(k, c)] = keep.tile([P, 4, 2], F32, name="ss%d%d" % (k, c))
                 st[(k, c)] = keep.tile([P, 2, 4], F32, name="st%d%d" % (k, c))
                 rc[(k, c)] = keep.tile([P, 2, 4], F32, name="rc%d%d" % (k, c))
-                sc[(k, c)] = keep.tile([P, 2, 4], F32, name="sc%d%d" % (k, c))
+                sc[(k, c)] = keep.tile([P, 4], F32, name="sc%d%d" % (k, c))
             for j in range(4):
                 o0[(k, j)] = keep.tile([P, 2, D], F32, name="o0%d%d" % (k, j))
                 o1[(k, j)] = keep.tile([P, 2, D], FP8, name="o1%d%d" % (k, j))
@@ -185,7 +185,7 @@ def tile_gat_pa_kernel(tc, x, W1, b1, W2, b2, W3, b3, out_0, out_1):
                 r = rows(j) + t
                 sq = junk.tile([P, D], BF16, tag="sq")
                 nc.scalar.activation(
-                    out=sq[:], in_=h[(k, j // 2)][:, r, :], func=ACT.Square, accum_out=ss[(k, j // 2)][:, r : r + 1]
+                    out=sq[:], in_=h[(k, j // 2)][:, r, :], func=ACT.Square, accum_out=ss[(k, j // 2)][:, r, 0:1]
                 )
 
         def absmax(k, c, r0, n):
@@ -198,17 +198,12 @@ def tile_gat_pa_kernel(tc, x, W1, b1, W2, b2, W3, b3, out_0, out_1):
             )
 
         def clamp(k, c, r0, n):
-            nc.vector.tensor_scalar(
-                out=st[(k, c)][:, 0, r0 : r0 + n], in0=ss[(k, c)][:, r0 : r0 + n], scalar1=1e-24, scalar2=None, op0=ALU.max
-            )
-
-        def recip(k, c, r0, n):
-            nc.vector.reciprocal(out=rc[(k, c)][:, :, r0 : r0 + n], in_=st[(k, c)][:, :, r0 : r0 + n])
+            nc.vector.tensor_reduce(out=st[(k, c)][:, 0, r0 : r0 + n], in_=ss[(k, c)][:, r0 : r0 + n, :], axis=AX.X, op=ALU.max)
 
         def factors(k, c, r0, n):
-            nc.scalar.activation(out=sc[(k, c)][:, 0, r0 : r0 + n], in_=rc[(k, c)][:, 0, r0 : r0 + n], func=ACT.Sqrt)
+            nc.scalar.activation(out=rc[(k, c)][:, :, r0 : r0 + n], in_=st[(k, c)][:, :, r0 : r0 + n], func=ACT.Abs_reciprocal_sqrt)
             nc.scalar.activation(
-                out=sc[(k, c)][:, 1, r0 : r0 + n], in_=rc[(k, c)][:, 1, r0 : r0 + n], func=ACT.Copy, scale=448.0
+                out=sc[(k, c)][:, r0 : r0 + n], in_=rc[(k, c)][:, 1, r0 : r0 + n], func=ACT.Square, scale=448.0**0.5
             )
 
         def scale_row(k, j, t, eng):
@@ -217,7 +212,7 @@ def tile_gat_pa_kernel(tc, x, W1, b1, W2, b2, W3, b3, out_0, out_1):
                 nc.vector.tensor_scalar(
                     out=o0[(k, j)][:, t, :],
                     in0=h[(k, j // 2)][:, r, :],
-                    scalar1=sc[(k, j // 2)][:, 0, r : r + 1],
+                    scalar1=rc[(k, j // 2)][:, 0, r : r + 1],
                     scalar2=None,
                     op0=ALU.mult,
                 )
@@ -225,14 +220,14 @@ def tile_gat_pa_kernel(tc, x, W1, b1, W2, b2, W3, b3, out_0, out_1):
                 nc.gpsimd.tensor_scalar(
                     out=o0[(k, j)][:, t, :],
                     in0=h[(k, j // 2)][:, r, :],
-                    scalar1=sc[(k, j // 2)][:, 0, r : r + 1],
+                    scalar1=rc[(k, j // 2)][:, 0, r : r + 1],
                     scalar2=0.0,
                     op0=ALU.mult,
                     op1=ALU.add,
                 )
             else:
                 nc.scalar.activation(
-                    out=o0[(k, j)][:, t, :], in_=h[(k, j // 2)][:, r, :], func=ACT.Copy, scale=sc[(k, j // 2)][:, 0, r : r + 1]
+                    out=o0[(k, j)][:, t, :], in_=h[(k, j // 2)][:, r, :], func=ACT.Copy, scale=rc[(k, j // 2)][:, 0, r : r + 1]
                 )
 
         def cast_row(k, j, t, eng):
@@ -241,7 +236,7 @@ def tile_gat_pa_kernel(tc, x, W1, b1, W2, b2, W3, b3, out_0, out_1):
                 nc.vector.tensor_scalar(
                     out=o1[(k, j)][:, t, :],
                     in0=h[(k, j // 2)][:, r, :],
-                    scalar1=sc[(k, j // 2)][:, 1, r : r + 1],
+                    scalar1=sc[(k, j // 2)][:, r : r + 1],
                     scalar2=None,
                     op0=ALU.mult,
                     saturate=False,
@@ -251,7 +246,7 @@ def tile_gat_pa_kernel(tc, x, W1, b1, W2, b2, W3, b3, out_0, out_1):
                     out=o1[(k, j)][:, t, :],
                     in_=h[(k, j // 2)][:, r, :],
                     func=ACT.Identity,
-                    scale=sc[(k, j // 2)][:, 1, r : r + 1],
+                    scale=sc[(k, j // 2)][:, r : r + 1],
                     bias=zero[:, 0:1],
                     saturate=False,
                 )
@@ -288,7 +283,10 @@ def tile_gat_pa_kernel(tc, x, W1, b1, W2, b2, W3, b3, out_0, out_1):
         nc.vector.memset(warm[:], 1.0)
         nc.vector.memset(ones[:], 1.0)
         nc.vector.memset(zero[:], 0.0)
-        nc.scalar.activation(out=warm2[:], in_=warm[:], func=ACT.Sqrt)
+        nc.scalar.activation(out=warm2[:], in_=warm[:], func=ACT.Abs_reciprocal_sqrt)
+        for k in range(HEADS):
+            for c in range(2):
+                nc.vector.memset(ss[(k, c)][:], 1e-24)
         make_identity(nc, ident[:])
         make_identity(nc, identb[:])
 
@@ -349,7 +347,6 @@ def tile_gat_pa_kernel(tc, x, W1, b1, W2, b2, W3, b3, out_0, out_1):
         w_copy(1, 1)
         add_bias(0, 2)
         sumsq(0, 2)
-        recip(0, 0, 0, 4)
         factors(0, 0, 0, 4)
         w_quant(1, 0)
         transposes(2, 0)
@@ -382,7 +379,6 @@ def tile_gat_pa_kernel(tc, x, W1, b1, W2, b2, W3, b3, out_0, out_1):
         scale_unit(units[1], "v")
         cast_unit(units[1])
         sumsq(1, 0)
-        recip(0, 1, 0, 4)
         factors(0, 1, 0, 4)
 
         for i in range(2, 5):
@@ -402,7 +398,6 @@ def tile_gat_pa_kernel(tc, x, W1, b1, W2, b2, W3, b3, out_0, out_1):
             sumsq(units[2 * i + 2][0], units[2 * i + 2][1])
             clamp(k, c, 0, 4)
             scale_unit(units[2 * i - 1], "v")
-            recip(k, c, 0, 4)
             factors(k, c, 0, 4)
 
         add_bias(2, 3)
@@ -412,14 +407,12 @@ def tile_gat_pa_kernel(tc, x, W1, b1, W2, b2, W3, b3, out_0, out_1):
         cast_unit(units[8])
         clamp(2, 1, 0, 2)
         absmax(2, 1, 2, 2)
-        recip(2, 1, 0, 2)
         factors(2, 1, 0, 2)
         scale_unit(units[9], "v")
         clamp(2, 1, 2, 2)
         cast_row(2, 1, 0, "v")
         cast_row(2, 1, 1, "v")
         store1(2, 1)
-        recip(2, 1, 2, 2)
         factors(2, 1, 2, 2)
         scale_unit(units[10], "v")
         cast_row(2, 2, 0, "s")

@@ -180,13 +180,16 @@ def tile_gat_pa_kernel(tc, x, W1, b1, W2, b2, W3, b3, out_0, out_1):
                 op=ALU.add,
             )
 
+        def sumsq_row(k, j, t):
+            r = rows(j) + t
+            sq = junk.tile([P, D], BF16, tag="sq")
+            nc.scalar.activation(
+                out=sq[:], in_=h[(k, j // 2)][:, r, :], func=ACT.Square, accum_out=ss[(k, j // 2)][:, r, 0:1]
+            )
+
         def sumsq(k, j):
-            for t in range(2):
-                r = rows(j) + t
-                sq = junk.tile([P, D], BF16, tag="sq")
-                nc.scalar.activation(
-                    out=sq[:], in_=h[(k, j // 2)][:, r, :], func=ACT.Square, accum_out=ss[(k, j // 2)][:, r, 0:1]
-                )
+            sumsq_row(k, j, 0)
+            sumsq_row(k, j, 1)
 
         def absmax(k, c, r0, n):
             nc.vector.tensor_reduce(
@@ -200,8 +203,10 @@ def tile_gat_pa_kernel(tc, x, W1, b1, W2, b2, W3, b3, out_0, out_1):
         def clamp(k, c, r0, n):
             nc.vector.tensor_reduce(out=st[(k, c)][:, 0, r0 : r0 + n], in_=ss[(k, c)][:, r0 : r0 + n, :], axis=AX.X, op=ALU.max)
 
-        def factors(k, c, r0, n):
+        def rsq(k, c, r0, n):
             nc.scalar.activation(out=rc[(k, c)][:, :, r0 : r0 + n], in_=st[(k, c)][:, :, r0 : r0 + n], func=ACT.Abs_reciprocal_sqrt)
+
+        def sq448(k, c, r0, n):
             nc.scalar.activation(
                 out=sc[(k, c)][:, r0 : r0 + n], in_=rc[(k, c)][:, 1, r0 : r0 + n], func=ACT.Square, scale=448.0**0.5
             )
@@ -347,11 +352,12 @@ def tile_gat_pa_kernel(tc, x, W1, b1, W2, b2, W3, b3, out_0, out_1):
         w_copy(1, 1)
         add_bias(0, 2)
         sumsq(0, 2)
-        factors(0, 0, 0, 4)
+        rsq(0, 0, 0, 4)
         w_quant(1, 0)
         transposes(2, 0)
         transposes(2, 1)
         w_copy(2, 0)
+        sq448(0, 0, 0, 4)
         w_copy(2, 1)
         add_bias(0, 3)
         sumsq(0, 3)
@@ -379,14 +385,16 @@ def tile_gat_pa_kernel(tc, x, W1, b1, W2, b2, W3, b3, out_0, out_1):
         scale_unit(units[1], "v")
         cast_unit(units[1])
         sumsq(1, 0)
-        factors(0, 1, 0, 4)
+        rsq(0, 1, 0, 4)
 
         for i in range(2, 5):
             u1 = units[2 * i + 1]
             k = u1[0]
             c = u1[1] // 2
             add_bias(u1[0], u1[1])
-            sumsq(u1[0], u1[1])
+            sumsq_row(u1[0], u1[1], 0)
+            sq448(units[2 * i - 2][0], units[2 * i - 2][1] // 2, 0, 4)
+            sumsq_row(u1[0], u1[1], 1)
             scale_unit(units[2 * i - 2], "g")
             cast_unit(units[2 * i - 2])
             cast_unit(units[2 * i - 1])
@@ -397,23 +405,27 @@ def tile_gat_pa_kernel(tc, x, W1, b1, W2, b2, W3, b3, out_0, out_1):
             add_bias(units[2 * i + 2][0], units[2 * i + 2][1])
             sumsq(units[2 * i + 2][0], units[2 * i + 2][1])
             clamp(k, c, 0, 4)
-            scale_unit(units[2 * i - 1], "v")
-            factors(k, c, 0, 4)
+            scale_unit(units[2 * i - 1], "g")
+            rsq(k, c, 0, 4)
 
         add_bias(2, 3)
-        sumsq(2, 3)
+        sumsq_row(2, 3, 0)
+        sq448(2, 0, 0, 4)
+        sumsq_row(2, 3, 1)
         absmax(2, 1, 0, 2)
         scale_unit(units[8], "v")
         cast_unit(units[8])
         clamp(2, 1, 0, 2)
         absmax(2, 1, 2, 2)
-        factors(2, 1, 0, 2)
+        rsq(2, 1, 0, 2)
+        sq448(2, 1, 0, 2)
         scale_unit(units[9], "v")
         clamp(2, 1, 2, 2)
         cast_row(2, 1, 0, "v")
         cast_row(2, 1, 1, "v")
         store1(2, 1)
-        factors(2, 1, 2, 2)
+        rsq(2, 1, 2, 2)
+        sq448(2, 1, 2, 2)
         scale_unit(units[10], "v")
         cast_row(2, 2, 0, "s")
         cast_row(2, 2, 1, "v")

@@ -75,9 +75,9 @@ def tile_gat_pa_kernel(tc, x, W1, b1, W2, b2, W3, b3, out_0, out_1):
                 st[(k, c)] = keep.tile([P, 2, 4], F32, name="st%d%d" % (k, c))
                 rc[(k, c)] = keep.tile([P, 2, 4], F32, name="rc%d%d" % (k, c))
                 sc[(k, c)] = keep.tile([P, 4], F32, name="sc%d%d" % (k, c))
+                o1[(k, c)] = keep.tile([P, 4, D], FP8, name="o1%d%d" % (k, c))
             for j in range(4):
                 o0[(k, j)] = keep.tile([P, 2, D], F32, name="o0%d%d" % (k, j))
-                o1[(k, j)] = keep.tile([P, 2, D], FP8, name="o1%d%d" % (k, j))
         tps = {}
         accs = {}
 
@@ -124,8 +124,8 @@ def tile_gat_pa_kernel(tc, x, W1, b1, W2, b2, W3, b3, out_0, out_1):
             nc.vector.quantize_mx(out=wc[(k, g)][:].bitcast(FP8X4), scales=ws[(k, g)][:], in_=wg[(k, g)][:])
 
         def x_interleave(g, j, eng):
-            src = xraw[(g, j // 2)][:, :, 256 * (j % 2) : 256 * (j % 2) + 256].rearrange("q j (c i) -> q c j i", i=4)
-            dst = xg[(g, j)][:].rearrange("q (c i) j -> q c j i", i=4)
+            src = xraw[(g, j // 2)][:, :, 256 * (j % 2) : 256 * (j % 2) + 256].rearrange("q j (p t) -> q t p j", t=2)
+            dst = xg[(g, j)][:].rearrange("q (t p) j -> q t p j", t=2)
             if eng == "v":
                 nc.vector.tensor_copy(out=dst, in_=src)
             else:
@@ -239,7 +239,7 @@ def tile_gat_pa_kernel(tc, x, W1, b1, W2, b2, W3, b3, out_0, out_1):
             r = rows(j) + t
             if eng == "v":
                 nc.vector.tensor_scalar(
-                    out=o1[(k, j)][:, t, :],
+                    out=o1[(k, j // 2)][:, r, :],
                     in0=h[(k, j // 2)][:, r, :],
                     scalar1=sc[(k, j // 2)][:, r : r + 1],
                     scalar2=None,
@@ -248,7 +248,7 @@ def tile_gat_pa_kernel(tc, x, W1, b1, W2, b2, W3, b3, out_0, out_1):
                 )
             else:
                 nc.scalar.activation(
-                    out=o1[(k, j)][:, t, :],
+                    out=o1[(k, j // 2)][:, r, :],
                     in_=h[(k, j // 2)][:, r, :],
                     func=ACT.Identity,
                     scale=sc[(k, j // 2)][:, r : r + 1],
@@ -258,15 +258,18 @@ def tile_gat_pa_kernel(tc, x, W1, b1, W2, b2, W3, b3, out_0, out_1):
 
         def node_view(ap, k, j):
             rows_of_unit = ap[k, 256 * j : 256 * (j + 1), :]
-            if j % 2 == 0:
-                return rows_of_unit.rearrange("(t p) d -> p t d", t=2)
             return rows_of_unit.rearrange("(p t) d -> p t d", t=2)
 
         def store0(k, j):
             nc.sync.dma_start(out=node_view(out_0, k, j), in_=o0[(k, j)][:])
 
         def store1(k, j):
-            nc.sync.dma_start(out=node_view(out_1, k, j), in_=o1[(k, j)][:].bitcast(U8))
+            if j % 2 == 1:
+                c = j // 2
+                nc.sync.dma_start(
+                    out=out_1[k, 512 * c : 512 * (c + 1), :].rearrange("(u p t) d -> p u (t d)", u=2, t=2),
+                    in_=o1[(k, c)][:].bitcast(U8).rearrange("p (u t) d -> p u (t d)", u=2),
+                )
 
         def finish_first(u, eng):
             scale_row(u[0], u[1], 0, eng)

@@ -18,6 +18,13 @@ FEAT = 1024
 NODES = 1024
 D = 256
 HEADS = 3
+PASSES = 2
+SLOTS = 4
+K_PASS = P * SLOTS
+UNIT = 256
+PAIR = 512
+FP8_MAX = 448.0
+NORM_FLOOR = 1e-12
 FLOPS = 2 * NODES * FEAT * D * HEADS
 
 
@@ -50,17 +57,17 @@ def tile_gat_pa_kernel(tc, x, W1, b1, W2, b2, W3, b3, out_0, out_1):
         xg = {}
         xc = {}
         xs = {}
-        for g in range(2):
+        for g in range(PASSES):
             for c in range(2):
-                xraw[(g, c)] = keep.tile([P, 4, 512], BF16, name="xraw%d%d" % (g, c))
+                xraw[(g, c)] = keep.tile([P, SLOTS, PAIR], BF16, name="xraw%d%d" % (g, c))
             for k in range(HEADS):
-                wg[(k, g)] = keep.tile([P, 4 * D], BF16, name="wg%d%d" % (k, g), align_bytes=64)
+                wg[(k, g)] = keep.tile([P, SLOTS * D], BF16, name="wg%d%d" % (k, g), align_bytes=64)
                 wc[(k, g)] = keep.tile([P, D], U32, name="wc%d%d" % (k, g), align_bytes=64)
                 ws[(k, g)] = keep.tile([P, D], U8, name="ws%d%d" % (k, g), align_bytes=64)
             for j in range(4):
-                xg[(g, j)] = keep.tile([P, 256, 4], BF16, name="xg%d%d" % (g, j), align_bytes=64)
-                xc[(g, j)] = keep.tile([P, 256], U32, name="xc%d%d" % (g, j), align_bytes=64)
-                xs[(g, j)] = keep.tile([P, 256], U8, name="xs%d%d" % (g, j), align_bytes=64)
+                xg[(g, j)] = keep.tile([P, UNIT, SLOTS], BF16, name="xg%d%d" % (g, j), align_bytes=64)
+                xc[(g, j)] = keep.tile([P, UNIT], U32, name="xc%d%d" % (g, j), align_bytes=64)
+                xs[(g, j)] = keep.tile([P, UNIT], U8, name="xs%d%d" % (g, j), align_bytes=64)
         h = {}
         ss = {}
         st = {}
@@ -78,8 +85,7 @@ def tile_gat_pa_kernel(tc, x, W1, b1, W2, b2, W3, b3, out_0, out_1):
                 o1[(k, c)] = keep.tile([P, 4, D], FP8, name="o1%d%d" % (k, c))
             for j in range(4):
                 o0[(k, j)] = keep.tile([P, 2, D], F32, name="o0%d%d" % (k, j))
-        tps = {}
-        accs = {}
+        banks = {}
 
         def load_w(k):
             nc.sync.dma_start(out=wraw[k][:], in_=weights[k].rearrange("(a p) f -> p a f", p=P))
@@ -91,7 +97,7 @@ def tile_gat_pa_kernel(tc, x, W1, b1, W2, b2, W3, b3, out_0, out_1):
         def load_x(g, c):
             nc.sync.dma_start(
                 out=xraw[(g, c)][:],
-                in_=xf[512 * g : 512 * (g + 1), 512 * c : 512 * (c + 1)].rearrange("(p j) w -> p j w", j=4),
+                in_=xf[K_PASS * g : K_PASS * (g + 1), PAIR * c : PAIR * (c + 1)].rearrange("(p s) w -> p s w", s=SLOTS),
             )
 
         def bias_matmul():
@@ -99,64 +105,63 @@ def tile_gat_pa_kernel(tc, x, W1, b1, W2, b2, W3, b3, out_0, out_1):
             nc.tensor.matmul(out=pb0[:], lhsT=ones[:], rhs=brow[:, 0:512], start=True, stop=True)
             pb1 = ps_a.tile([P, 512], F32, tag="acc")
             nc.tensor.matmul(out=pb1[:, 0:256], lhsT=ones[:], rhs=brow[:, 512:768], start=True, stop=True)
-            accs["b0"] = pb0
-            accs["b1"] = pb1
+            banks["b0"] = pb0
+            banks["b1"] = pb1
 
         def bias_copy():
-            nc.scalar.copy(out=bias[:, 0:512], in_=accs["b0"][:])
-            nc.scalar.copy(out=bias[:, 512:768], in_=accs["b1"][:, 0:256])
+            nc.scalar.copy(out=bias[:, 0:512], in_=banks["b0"][:])
+            nc.scalar.copy(out=bias[:, 512:768], in_=banks["b1"][:, 0:256])
 
-        def transposes(k, g):
+        def w_transposes(k, g):
             tp = ps_t.tile([P, 4, P], F32, tag="tp")
             for a in range(2):
                 words = wraw[k][:, a, :].bitcast(F32)
                 for u in range(2):
                     nc.tensor.transpose(tp[:, 2 * a + u, :], words[:, 256 * g + u : 256 * (g + 1) : 2], ident[:])
-            tps[(k, g)] = tp
+            banks[("w", k, g)] = tp
 
         def w_copy(k, g):
             nc.scalar.copy(
                 out=wg[(k, g)][:].bitcast(F32).rearrange("p (a r u) -> p a r u", a=2, u=2),
-                in_=tps[(k, g)][:].rearrange("p (a u) r -> p a r u", u=2),
+                in_=banks[("w", k, g)][:].rearrange("p (a u) r -> p a r u", u=2),
             )
 
         def w_quant(k, g):
             nc.vector.quantize_mx(out=wc[(k, g)][:].bitcast(FP8X4), scales=ws[(k, g)][:], in_=wg[(k, g)][:])
 
-        def x_interleave(g, j, eng):
-            src = xraw[(g, j // 2)][:, :, 256 * (j % 2) : 256 * (j % 2) + 256].rearrange("q j (p t) -> q t p j", t=2)
-            dst = xg[(g, j)][:].rearrange("q (t p) j -> q t p j", t=2)
-            if eng == "v":
-                nc.vector.tensor_copy(out=dst, in_=src)
-            else:
-                nc.scalar.copy(out=dst, in_=src)
+        def unit_columns(g, j):
+            return xraw[(g, j // 2)][:, :, UNIT * (j % 2) : UNIT * (j % 2) + UNIT]
+
+        def x_interleave(g, j):
+            nc.vector.tensor_copy(
+                out=xg[(g, j)][:].rearrange("q (t p) s -> q t p s", t=2),
+                in_=unit_columns(g, j).rearrange("q s (p t) -> q t p s", t=2),
+            )
 
         def pe_interleave(g, j):
-            pil = ps_a.tile([P, 1024], BF16, tag="acc")
+            pil = ps_a.tile([P, SLOTS * UNIT], BF16, tag="acc")
             for u in range(2):
                 nc.tensor.matmul(
                     out=pil[:].rearrange("q (t p u e) -> q u t p e", t=2, u=2, e=2)[:, u],
                     lhsT=identb[:],
-                    rhs=xraw[(g, j // 2)][:, 2 * u : 2 * u + 2, 256 * (j % 2) : 256 * (j % 2) + 256].rearrange(
-                        "q e (p t) -> q t p e", t=2
-                    ),
+                    rhs=unit_columns(g, j)[:, 2 * u : 2 * u + 2, :].rearrange("q e (p t) -> q t p e", t=2),
                     start=True,
                     stop=True,
                 )
-            accs[("x", g, j)] = pil
+            banks[("x", g, j)] = pil
 
         def x_copy(g, j):
-            nc.scalar.copy(out=xg[(g, j)][:].rearrange("q w j -> q (w j)"), in_=accs[("x", g, j)][:])
+            nc.scalar.copy(out=xg[(g, j)][:].rearrange("q w s -> q (w s)"), in_=banks[("x", g, j)][:])
 
         def x_quant(g, j):
             nc.vector.quantize_mx(
-                out=xc[(g, j)][:].bitcast(FP8X4), scales=xs[(g, j)][:], in_=xg[(g, j)][:].rearrange("p w j -> p (w j)")
+                out=xc[(g, j)][:].bitcast(FP8X4), scales=xs[(g, j)][:], in_=xg[(g, j)][:].rearrange("p w s -> p (w s)")
             )
 
         def mm(k, j):
             acc = ps_a.tile([P, 2, D], F32, tag="acc")
             for t in range(2):
-                for g in range(2):
+                for g in range(PASSES):
                     nc.tensor.matmul_mx(
                         out=acc[:, t, :],
                         lhsT=xc[(g, j)][:, P * t : P * (t + 1)].bitcast(FP8X4),
@@ -164,24 +169,24 @@ def tile_gat_pa_kernel(tc, x, W1, b1, W2, b2, W3, b3, out_0, out_1):
                         rhs=wc[(k, g)][:].bitcast(FP8X4),
                         rhs_scale=ws[(k, g)][:],
                         start=(g == 0),
-                        stop=(g == 1),
+                        stop=(g == PASSES - 1),
                     )
-            accs[(k, j)] = acc
+            banks[(k, j)] = acc
 
-        def rows(j):
+        def first_row(j):
             return 2 * (j % 2)
 
         def add_bias(k, j):
-            r = rows(j)
+            r = first_row(j)
             nc.vector.tensor_tensor(
                 out=h[(k, j // 2)][:, r : r + 2, :],
-                in0=accs[(k, j)][:],
+                in0=banks[(k, j)][:],
                 in1=bias[:, D * k : D * (k + 1)].unsqueeze(1).to_broadcast([P, 2, D]),
                 op=ALU.add,
             )
 
         def sumsq_row(k, j, t):
-            r = rows(j) + t
+            r = first_row(j) + t
             sq = junk.tile([P, D], BF16, tag="sq")
             nc.scalar.activation(
                 out=sq[:], in_=h[(k, j // 2)][:, r, :], func=ACT.Square, accum_out=ss[(k, j // 2)][:, r, 0:1]
@@ -200,92 +205,82 @@ def tile_gat_pa_kernel(tc, x, W1, b1, W2, b2, W3, b3, out_0, out_1):
                 apply_absolute_value=True,
             )
 
-        def clamp(k, c, r0, n):
+        def floor_sumsq(k, c, r0, n):
             nc.vector.tensor_reduce(out=st[(k, c)][:, 0, r0 : r0 + n], in_=ss[(k, c)][:, r0 : r0 + n, :], axis=AX.X, op=ALU.max)
 
-        def rsq(k, c, r0, n):
+        def rsqrt_stats(k, c, r0, n):
             nc.scalar.activation(out=rc[(k, c)][:, :, r0 : r0 + n], in_=st[(k, c)][:, :, r0 : r0 + n], func=ACT.Abs_reciprocal_sqrt)
 
-        def sq448(k, c, r0, n):
+        def cast_factor(k, c, r0, n):
             nc.scalar.activation(
-                out=sc[(k, c)][:, r0 : r0 + n], in_=rc[(k, c)][:, 1, r0 : r0 + n], func=ACT.Square, scale=448.0**0.5
+                out=sc[(k, c)][:, r0 : r0 + n], in_=rc[(k, c)][:, 1, r0 : r0 + n], func=ACT.Square, scale=FP8_MAX**0.5
             )
 
-        def scale_row(k, j, t, eng):
-            r = rows(j) + t
-            if eng == "v":
-                nc.vector.tensor_scalar(
-                    out=o0[(k, j)][:, t, :],
-                    in0=h[(k, j // 2)][:, r, :],
-                    scalar1=rc[(k, j // 2)][:, 0, r : r + 1],
-                    scalar2=None,
-                    op0=ALU.mult,
-                )
-            elif eng == "g":
-                nc.gpsimd.tensor_scalar(
-                    out=o0[(k, j)][:, t, :],
-                    in0=h[(k, j // 2)][:, r, :],
-                    scalar1=rc[(k, j // 2)][:, 0, r : r + 1],
-                    scalar2=0.0,
-                    op0=ALU.mult,
-                    op1=ALU.add,
-                )
-            else:
-                nc.scalar.activation(
-                    out=o0[(k, j)][:, t, :], in_=h[(k, j // 2)][:, r, :], func=ACT.Copy, scale=rc[(k, j // 2)][:, 0, r : r + 1]
-                )
+        def scale_row_vector(k, j, t):
+            r = first_row(j) + t
+            nc.vector.tensor_scalar(
+                out=o0[(k, j)][:, t, :],
+                in0=h[(k, j // 2)][:, r, :],
+                scalar1=rc[(k, j // 2)][:, 0, r : r + 1],
+                scalar2=None,
+                op0=ALU.mult,
+            )
 
-        def cast_row(k, j, t, eng):
-            r = rows(j) + t
-            if eng == "v":
-                nc.vector.tensor_scalar(
-                    out=o1[(k, j // 2)][:, r, :],
-                    in0=h[(k, j // 2)][:, r, :],
-                    scalar1=sc[(k, j // 2)][:, r : r + 1],
-                    scalar2=None,
-                    op0=ALU.mult,
-                    saturate=False,
-                )
-            else:
-                nc.scalar.activation(
-                    out=o1[(k, j // 2)][:, r, :],
-                    in_=h[(k, j // 2)][:, r, :],
-                    func=ACT.Identity,
-                    scale=sc[(k, j // 2)][:, r : r + 1],
-                    bias=zero[:, 0:1],
-                    saturate=False,
-                )
+        def scale_row_gpsimd(k, j, t):
+            r = first_row(j) + t
+            nc.gpsimd.tensor_scalar(
+                out=o0[(k, j)][:, t, :],
+                in0=h[(k, j // 2)][:, r, :],
+                scalar1=rc[(k, j // 2)][:, 0, r : r + 1],
+                scalar2=0.0,
+                op0=ALU.mult,
+                op1=ALU.add,
+            )
 
-        def node_view(ap, k, j):
-            rows_of_unit = ap[k, 256 * j : 256 * (j + 1), :]
-            return rows_of_unit.rearrange("(p t) d -> p t d", t=2)
+        def cast_row_vector(k, j, t):
+            r = first_row(j) + t
+            nc.vector.tensor_scalar(
+                out=o1[(k, j // 2)][:, r, :],
+                in0=h[(k, j // 2)][:, r, :],
+                scalar1=sc[(k, j // 2)][:, r : r + 1],
+                scalar2=None,
+                op0=ALU.mult,
+                saturate=False,
+            )
 
-        def store0(k, j):
-            nc.sync.dma_start(out=node_view(out_0, k, j), in_=o0[(k, j)][:])
+        def cast_row_scalar(k, j, t):
+            r = first_row(j) + t
+            nc.scalar.activation(
+                out=o1[(k, j // 2)][:, r, :],
+                in_=h[(k, j // 2)][:, r, :],
+                func=ACT.Identity,
+                scale=sc[(k, j // 2)][:, r : r + 1],
+                bias=zero[:, 0:1],
+                saturate=False,
+            )
 
-        def store1(k, j):
-            if j % 2 == 1:
-                c = j // 2
-                nc.sync.dma_start(
-                    out=out_1[k, 512 * c : 512 * (c + 1), :].rearrange("(u p t) d -> p u (t d)", u=2, t=2),
-                    in_=o1[(k, c)][:].bitcast(U8).rearrange("p (u t) d -> p u (t d)", u=2),
-                )
+        def store_unit(k, j):
+            nc.sync.dma_start(out=out_0[k, UNIT * j : UNIT * (j + 1), :].rearrange("(p t) d -> p t d", t=2), in_=o0[(k, j)][:])
 
-        def finish_first(u, eng):
-            scale_row(u[0], u[1], 0, eng)
-            scale_row(u[0], u[1], 1, eng)
-            store0(u[0], u[1])
-            cast_row(u[0], u[1], 0, "s")
-            cast_row(u[0], u[1], 1, "s")
-            store1(u[0], u[1])
+        def store_bytes(k, c):
+            nc.sync.dma_start(
+                out=out_1[k, PAIR * c : PAIR * (c + 1), :].rearrange("(u p t) d -> p u (t d)", u=2, t=2),
+                in_=o1[(k, c)][:].bitcast(U8).rearrange("p (u t) d -> p u (t d)", u=2),
+            )
 
-        def finish_second(u, eng):
-            scale_row(u[0], u[1], 0, eng)
-            scale_row(u[0], u[1], 1, eng)
-            store0(u[0], u[1])
-            cast_row(u[0], u[1], 0, "s")
-            cast_row(u[0], u[1], 1, "s")
-            store1(u[0], u[1])
+        def scale_unit_vector(k, j):
+            scale_row_vector(k, j, 0)
+            scale_row_vector(k, j, 1)
+            store_unit(k, j)
+
+        def scale_unit_gpsimd(k, j):
+            scale_row_gpsimd(k, j, 0)
+            scale_row_gpsimd(k, j, 1)
+            store_unit(k, j)
+
+        def cast_unit_scalar(k, j):
+            cast_row_scalar(k, j, 0)
+            cast_row_scalar(k, j, 1)
 
         nc.vector.memset(brow[:], 0.0)
         nc.vector.memset(warm[:], 1.0)
@@ -294,7 +289,7 @@ def tile_gat_pa_kernel(tc, x, W1, b1, W2, b2, W3, b3, out_0, out_1):
         nc.scalar.activation(out=warm2[:], in_=warm[:], func=ACT.Abs_reciprocal_sqrt)
         for k in range(HEADS):
             for c in range(2):
-                nc.vector.memset(ss[(k, c)][:], 1e-24)
+                nc.vector.memset(ss[(k, c)][:], NORM_FLOOR**2)
         make_identity(nc, ident[:])
         make_identity(nc, identb[:])
 
@@ -307,23 +302,23 @@ def tile_gat_pa_kernel(tc, x, W1, b1, W2, b2, W3, b3, out_0, out_1):
         load_w(1)
         load_w(2)
 
-        transposes(0, 0)
-        transposes(0, 1)
+        w_transposes(0, 0)
+        w_transposes(0, 1)
         bias_matmul()
         pe_interleave(0, 1)
         w_copy(0, 0)
-        x_interleave(0, 0, "v")
+        x_interleave(0, 0)
         w_quant(0, 0)
         x_quant(0, 0)
         w_copy(0, 1)
         bias_copy()
         x_copy(0, 1)
         pe_interleave(1, 1)
-        x_interleave(1, 0, "v")
+        x_interleave(1, 0)
         w_quant(0, 1)
         x_quant(1, 0)
         x_copy(1, 1)
-        x_interleave(0, 2, "v")
+        x_interleave(0, 2)
         x_quant(0, 1)
         mm(0, 0)
         pe_interleave(0, 3)
@@ -331,10 +326,8 @@ def tile_gat_pa_kernel(tc, x, W1, b1, W2, b2, W3, b3, out_0, out_1):
         x_quant(0, 2)
         x_quant(1, 1)
         mm(0, 1)
-        x_interleave(1, 2, "v")
+        x_interleave(1, 2)
         pe_interleave(1, 3)
-
-        units = [(k, j) for k in range(HEADS) for j in range(4)]
 
         add_bias(0, 0)
         x_quant(1, 2)
@@ -346,94 +339,86 @@ def tile_gat_pa_kernel(tc, x, W1, b1, W2, b2, W3, b3, out_0, out_1):
         absmax(0, 0, 0, 2)
         absmax(0, 0, 2, 2)
         x_quant(1, 3)
-        transposes(1, 0)
-        transposes(1, 1)
+        w_transposes(1, 0)
+        w_transposes(1, 1)
         mm(0, 2)
         mm(0, 3)
-        clamp(0, 0, 0, 4)
+        floor_sumsq(0, 0, 0, 4)
         w_copy(1, 0)
         w_copy(1, 1)
         add_bias(0, 2)
         sumsq(0, 2)
-        rsq(0, 0, 0, 4)
+        rsqrt_stats(0, 0, 0, 4)
         w_quant(1, 0)
-        transposes(2, 0)
-        transposes(2, 1)
+        w_transposes(2, 0)
+        w_transposes(2, 1)
         w_copy(2, 0)
-        sq448(0, 0, 0, 4)
+        cast_factor(0, 0, 0, 4)
         w_copy(2, 1)
         add_bias(0, 3)
         sumsq(0, 3)
         w_quant(1, 1)
-        finish_first(units[0], "g")
+        scale_unit_gpsimd(0, 0)
+        cast_unit_scalar(0, 0)
         absmax(0, 1, 0, 2)
         absmax(0, 1, 2, 2)
         w_quant(2, 0)
         w_quant(2, 1)
         mm(1, 0)
         mm(1, 1)
-
-        def scale_unit(u, eng):
-            scale_row(u[0], u[1], 0, eng)
-            scale_row(u[0], u[1], 1, eng)
-            store0(u[0], u[1])
-
-        def cast_unit(u):
-            cast_row(u[0], u[1], 0, "s")
-            cast_row(u[0], u[1], 1, "s")
-            store1(u[0], u[1])
-
         add_bias(1, 0)
-        clamp(0, 1, 0, 4)
-        scale_unit(units[1], "v")
-        cast_unit(units[1])
+        floor_sumsq(0, 1, 0, 4)
+        scale_unit_vector(0, 1)
+        cast_unit_scalar(0, 1)
+        store_bytes(0, 0)
         sumsq(1, 0)
-        rsq(0, 1, 0, 4)
+        rsqrt_stats(0, 1, 0, 4)
 
+        pairs = [(k, c) for k in range(HEADS) for c in range(2)]
         for i in range(2, 5):
-            u1 = units[2 * i + 1]
-            k = u1[0]
-            c = u1[1] // 2
-            add_bias(u1[0], u1[1])
-            sumsq_row(u1[0], u1[1], 0)
-            sq448(units[2 * i - 2][0], units[2 * i - 2][1] // 2, 0, 4)
-            sumsq_row(u1[0], u1[1], 1)
-            scale_unit(units[2 * i - 2], "g")
-            cast_unit(units[2 * i - 2])
-            cast_unit(units[2 * i - 1])
+            k, c = pairs[i]
+            kp, cp = pairs[i - 1]
+            kn, cn = pairs[i + 1]
+            add_bias(k, 2 * c + 1)
+            sumsq_row(k, 2 * c + 1, 0)
+            cast_factor(kp, cp, 0, 4)
+            sumsq_row(k, 2 * c + 1, 1)
+            scale_unit_gpsimd(kp, 2 * cp)
+            cast_unit_scalar(kp, 2 * cp)
+            cast_unit_scalar(kp, 2 * cp + 1)
+            store_bytes(kp, cp)
             absmax(k, c, 0, 2)
             absmax(k, c, 2, 2)
-            mm(units[2 * i + 2][0], units[2 * i + 2][1])
-            mm(units[2 * i + 3][0], units[2 * i + 3][1])
-            add_bias(units[2 * i + 2][0], units[2 * i + 2][1])
-            sumsq(units[2 * i + 2][0], units[2 * i + 2][1])
-            clamp(k, c, 0, 4)
-            scale_unit(units[2 * i - 1], "g")
-            rsq(k, c, 0, 4)
+            mm(kn, 2 * cn)
+            mm(kn, 2 * cn + 1)
+            add_bias(kn, 2 * cn)
+            sumsq(kn, 2 * cn)
+            floor_sumsq(k, c, 0, 4)
+            scale_unit_gpsimd(kp, 2 * cp + 1)
+            rsqrt_stats(k, c, 0, 4)
 
         add_bias(2, 3)
         sumsq_row(2, 3, 0)
-        sq448(2, 0, 0, 4)
+        cast_factor(2, 0, 0, 4)
         sumsq_row(2, 3, 1)
         absmax(2, 1, 0, 2)
-        scale_unit(units[8], "v")
-        cast_unit(units[8])
-        clamp(2, 1, 0, 2)
+        scale_unit_vector(2, 0)
+        cast_unit_scalar(2, 0)
+        floor_sumsq(2, 1, 0, 2)
         absmax(2, 1, 2, 2)
-        rsq(2, 1, 0, 2)
-        sq448(2, 1, 0, 2)
-        scale_unit(units[9], "v")
-        clamp(2, 1, 2, 2)
-        cast_row(2, 1, 0, "v")
-        cast_row(2, 1, 1, "v")
-        store1(2, 1)
-        rsq(2, 1, 2, 2)
-        sq448(2, 1, 2, 2)
-        scale_unit(units[10], "v")
-        cast_row(2, 2, 0, "s")
-        cast_row(2, 2, 1, "v")
-        store1(2, 2)
-        scale_unit(units[11], "v")
-        cast_row(2, 3, 0, "s")
-        cast_row(2, 3, 1, "v")
-        store1(2, 3)
+        rsqrt_stats(2, 1, 0, 2)
+        cast_factor(2, 1, 0, 2)
+        scale_unit_vector(2, 1)
+        floor_sumsq(2, 1, 2, 2)
+        cast_row_vector(2, 1, 0)
+        cast_row_vector(2, 1, 1)
+        store_bytes(2, 0)
+        rsqrt_stats(2, 1, 2, 2)
+        cast_factor(2, 1, 2, 2)
+        scale_unit_vector(2, 2)
+        cast_row_scalar(2, 2, 0)
+        cast_row_vector(2, 2, 1)
+        scale_unit_vector(2, 3)
+        cast_row_scalar(2, 3, 0)
+        cast_row_vector(2, 3, 1)
+        store_bytes(2, 1)

from contextlib import ExitStack

import concourse.mybir as mybir
from concourse.masks import make_identity

F32 = mybir.dt.float32
BF16 = mybir.dt.bfloat16
U32 = mybir.dt.uint32
U8 = mybir.dt.uint8
FP8X4 = mybir.dt.float8_e4m3fn_x4
FP8 = mybir.dt.float8_e4m3fn
ALU = mybir.AluOpType
ACT = mybir.ActivationFunctionType
AX = mybir.AxisListType

P = 128
FEAT = 1024
NODES = 1024
D = 256
HEADS = 3
PASSES = 2
SLOTS = 4
K_PASS = P * SLOTS
UNIT = 256
PAIR = 512
FP8_MAX = 448.0
NORM_FLOOR = 1e-12
FLOPS = 2 * NODES * FEAT * D * HEADS


def tile_gat_pa_kernel(tc, x, W1, b1, W2, b2, W3, b3, out_0, out_1):
    nc = tc.nc
    weights = (W1, W2, W3)
    biases = (b1, b2, b3)
    xf = x.rearrange("b f h w -> (b f) (h w)")

    with ExitStack() as ctx:
        keep = ctx.enter_context(tc.tile_pool(name="keep", bufs=1))
        junk = ctx.enter_context(tc.tile_pool(name="junk", bufs=2))
        ps_t = ctx.enter_context(tc.psum_pool(name="ps_t", bufs=2))
        ps_a = ctx.enter_context(tc.psum_pool(name="ps_a", bufs=6))
        ctx.enter_context(tc.manual_schedule())

        brow = keep.tile([P, HEADS * D], BF16, name="brow")
        ones = keep.tile([P, P], BF16, name="ones")
        warm = keep.tile([P, 1], F32, name="warm")
        warm2 = keep.tile([P, 1], F32, name="warm2")
        zero = keep.tile([P, 1], F32, name="zero")
        ident = keep.tile([P, P], F32, name="ident")
        identb = keep.tile([P, P], BF16, name="identb")
        bias = keep.tile([P, HEADS * D], F32, name="bias")
        wraw = [keep.tile([P, 2, FEAT], BF16, name="wraw%d" % k) for k in range(HEADS)]
        xraw = {}
        wg = {}
        wc = {}
        ws = {}
        xg = {}
        xc = {}
        xs = {}
        for g in range(PASSES):
            for c in range(2):
                xraw[(g, c)] = keep.tile([P, SLOTS, PAIR], BF16, name="xraw%d%d" % (g, c))
            for k in range(HEADS):
                wg[(k, g)] = keep.tile([P, SLOTS * D], BF16, name="wg%d%d" % (k, g), align_bytes=64)
                wc[(k, g)] = keep.tile([P, D], U32, name="wc%d%d" % (k, g), align_bytes=64)
                ws[(k, g)] = keep.tile([P, D], U8, name="ws%d%d" % (k, g), align_bytes=64)
            for j in range(4):
                xg[(g, j)] = keep.tile([P, UNIT, SLOTS], BF16, name="xg%d%d" % (g, j), align_bytes=64)
                xc[(g, j)] = keep.tile([P, UNIT], U32, name="xc%d%d" % (g, j), align_bytes=64)
                xs[(g, j)] = keep.tile([P, UNIT], U8, name="xs%d%d" % (g, j), align_bytes=64)
        h = {}
        ss = {}
        st = {}
        rc = {}
        sc = {}
        o0 = {}
        o1 = {}
        for k in range(HEADS):
            for c in range(2):
                h[(k, c)] = keep.tile([P, 4, D], F32, name="h%d%d" % (k, c))
                ss[(k, c)] = keep.tile([P, 4, 2], F32, name="ss%d%d" % (k, c))
                st[(k, c)] = keep.tile([P, 2, 4], F32, name="st%d%d" % (k, c))
                rc[(k, c)] = keep.tile([P, 2, 4], F32, name="rc%d%d" % (k, c))
                sc[(k, c)] = keep.tile([P, 4], F32, name="sc%d%d" % (k, c))
                o1[(k, c)] = keep.tile([P, 4, D], FP8, name="o1%d%d" % (k, c))
            for j in range(4):
                o0[(k, j)] = keep.tile([P, 2, D], F32, name="o0%d%d" % (k, j))
        banks = {}

        def load_w(k):
            nc.sync.dma_start(out=wraw[k][:], in_=weights[k].rearrange("(a p) f -> p a f", p=P))

        def load_bias():
            for k in range(HEADS):
                nc.sync.dma_start(out=brow[0:1, D * k : D * (k + 1)], in_=biases[k].rearrange("(o d) -> o d", o=1))

        def load_x(g, c):
            nc.sync.dma_start(
                out=xraw[(g, c)][:],
                in_=xf[K_PASS * g : K_PASS * (g + 1), PAIR * c : PAIR * (c + 1)].rearrange("(p s) w -> p s w", s=SLOTS),
            )

        def bias_matmul():
            pb0 = ps_a.tile([P, 512], F32, tag="acc")
            nc.tensor.matmul(out=pb0[:], lhsT=ones[:], rhs=brow[:, 0:512], start=True, stop=True)
            pb1 = ps_a.tile([P, 512], F32, tag="acc")
            nc.tensor.matmul(out=pb1[:, 0:256], lhsT=ones[:], rhs=brow[:, 512:768], start=True, stop=True)
            banks["b0"] = pb0
            banks["b1"] = pb1

        def bias_copy():
            nc.scalar.copy(out=bias[:, 0:512], in_=banks["b0"][:])
            nc.scalar.copy(out=bias[:, 512:768], in_=banks["b1"][:, 0:256])

        def w_transposes(k, g):
            tp = ps_t.tile([P, 4, P], F32, tag="tp")
            for a in range(2):
                words = wraw[k][:, a, :].bitcast(F32)
                for u in range(2):
                    nc.tensor.transpose(tp[:, 2 * a + u, :], words[:, 256 * g + u : 256 * (g + 1) : 2], ident[:])
            banks[("w", k, g)] = tp

        def w_copy(k, g):
            nc.scalar.copy(
                out=wg[(k, g)][:].bitcast(F32).rearrange("p (a r u) -> p a r u", a=2, u=2),
                in_=banks[("w", k, g)][:].rearrange("p (a u) r -> p a r u", u=2),
            )

        def w_quant(k, g):
            nc.vector.quantize_mx(out=wc[(k, g)][:].bitcast(FP8X4), scales=ws[(k, g)][:], in_=wg[(k, g)][:])

        def unit_columns(g, j):
            return xraw[(g, j // 2)][:, :, UNIT * (j % 2) : UNIT * (j % 2) + UNIT]

        def x_interleave(g, j):
            nc.vector.tensor_copy(
                out=xg[(g, j)][:].rearrange("q (t p) s -> q t p s", t=2),
                in_=unit_columns(g, j).rearrange("q s (p t) -> q t p s", t=2),
            )

        def pe_interleave(g, j):
            pil = ps_a.tile([P, SLOTS * UNIT], BF16, tag="acc")
            for u in range(2):
                nc.tensor.matmul(
                    out=pil[:].rearrange("q (t p u e) -> q u t p e", t=2, u=2, e=2)[:, u],
                    lhsT=identb[:],
                    rhs=unit_columns(g, j)[:, 2 * u : 2 * u + 2, :].rearrange("q e (p t) -> q t p e", t=2),
                    start=True,
                    stop=True,
                )
            banks[("x", g, j)] = pil

        def x_copy(g, j):
            nc.scalar.copy(out=xg[(g, j)][:].rearrange("q w s -> q (w s)"), in_=banks[("x", g, j)][:])

        def x_quant(g, j):
            nc.vector.quantize_mx(
                out=xc[(g, j)][:].bitcast(FP8X4), scales=xs[(g, j)][:], in_=xg[(g, j)][:].rearrange("p w s -> p (w s)")
            )

        def mm(k, j):
            acc = ps_a.tile([P, 2, D], F32, tag="acc")
            for t in range(2):
                for g in range(PASSES):
                    nc.tensor.matmul_mx(
                        out=acc[:, t, :],
                        lhsT=xc[(g, j)][:, P * t : P * (t + 1)].bitcast(FP8X4),
                        lhsT_scale=xs[(g, j)][:, P * t : P * (t + 1)],
                        rhs=wc[(k, g)][:].bitcast(FP8X4),
                        rhs_scale=ws[(k, g)][:],
                        start=(g == 0),
                        stop=(g == PASSES - 1),
                    )
            banks[(k, j)] = acc

        def first_row(j):
            return 2 * (j % 2)

        def add_bias(k, j):
            r = first_row(j)
            nc.vector.tensor_tensor(
                out=h[(k, j // 2)][:, r : r + 2, :],
                in0=banks[(k, j)][:],
                in1=bias[:, D * k : D * (k + 1)].unsqueeze(1).to_broadcast([P, 2, D]),
                op=ALU.add,
            )

        def sumsq_row(k, j, t):
            r = first_row(j) + t
            sq = junk.tile([P, D], BF16, tag="sq")
            nc.scalar.activation(
                out=sq[:], in_=h[(k, j // 2)][:, r, :], func=ACT.Square, accum_out=ss[(k, j // 2)][:, r, 0:1]
            )

        def sumsq(k, j):
            sumsq_row(k, j, 0)
            sumsq_row(k, j, 1)

        def absmax(k, c, r0, n):
            nc.vector.tensor_reduce(
                out=st[(k, c)][:, 1, r0 : r0 + n],
                in_=h[(k, c)][:, r0 : r0 + n, :],
                axis=AX.X,
                op=ALU.max,
                apply_absolute_value=True,
            )

        def floor_sumsq(k, c, r0, n):
            nc.vector.tensor_reduce(out=st[(k, c)][:, 0, r0 : r0 + n], in_=ss[(k, c)][:, r0 : r0 + n, :], axis=AX.X, op=ALU.max)

        def rsqrt_stats(k, c, r0, n):
            nc.scalar.activation(out=rc[(k, c)][:, :, r0 : r0 + n], in_=st[(k, c)][:, :, r0 : r0 + n], func=ACT.Abs_reciprocal_sqrt)

        def cast_factor(k, c, r0, n):
            nc.scalar.activation(
                out=sc[(k, c)][:, r0 : r0 + n], in_=rc[(k, c)][:, 1, r0 : r0 + n], func=ACT.Square, scale=FP8_MAX**0.5
            )

        def scale_row_vector(k, j, t):
            r = first_row(j) + t
            nc.vector.tensor_scalar(
                out=o0[(k, j)][:, t, :],
                in0=h[(k, j // 2)][:, r, :],
                scalar1=rc[(k, j // 2)][:, 0, r : r + 1],
                scalar2=None,
                op0=ALU.mult,
            )

        def scale_row_gpsimd(k, j, t):
            r = first_row(j) + t
            nc.gpsimd.tensor_scalar(
                out=o0[(k, j)][:, t, :],
                in0=h[(k, j // 2)][:, r, :],
                scalar1=rc[(k, j // 2)][:, 0, r : r + 1],
                scalar2=0.0,
                op0=ALU.mult,
                op1=ALU.add,
            )

        def cast_row_vector(k, j, t):
            r = first_row(j) + t
            nc.vector.tensor_scalar(
                out=o1[(k, j // 2)][:, r, :],
                in0=h[(k, j // 2)][:, r, :],
                scalar1=sc[(k, j // 2)][:, r : r + 1],
                scalar2=None,
                op0=ALU.mult,
                saturate=False,
            )

        def cast_row_scalar(k, j, t):
            r = first_row(j) + t
            nc.scalar.activation(
                out=o1[(k, j // 2)][:, r, :],
                in_=h[(k, j // 2)][:, r, :],
                func=ACT.Identity,
                scale=sc[(k, j // 2)][:, r : r + 1],
                bias=zero[:, 0:1],
                saturate=False,
            )

        def store_unit(k, j):
            nc.sync.dma_start(out=out_0[k, UNIT * j : UNIT * (j + 1), :].rearrange("(p t) d -> p t d", t=2), in_=o0[(k, j)][:])

        def store_bytes(k, c):
            nc.sync.dma_start(
                out=out_1[k, PAIR * c : PAIR * (c + 1), :].rearrange("(u p t) d -> p u (t d)", u=2, t=2),
                in_=o1[(k, c)][:].bitcast(U8).rearrange("p (u t) d -> p u (t d)", u=2),
            )

        def scale_unit_vector(k, j):
            scale_row_vector(k, j, 0)
            scale_row_vector(k, j, 1)
            store_unit(k, j)

        def scale_unit_gpsimd(k, j):
            scale_row_gpsimd(k, j, 0)
            scale_row_gpsimd(k, j, 1)
            store_unit(k, j)

        def cast_unit_scalar(k, j):
            cast_row_scalar(k, j, 0)
            cast_row_scalar(k, j, 1)

        nc.vector.memset(brow[:], 0.0)
        nc.vector.memset(warm[:], 1.0)
        nc.vector.memset(ones[:], 1.0)
        nc.vector.memset(zero[:], 0.0)
        nc.scalar.activation(out=warm2[:], in_=warm[:], func=ACT.Abs_reciprocal_sqrt)
        for k in range(HEADS):
            for c in range(2):
                nc.vector.memset(ss[(k, c)][:], NORM_FLOOR**2)
        make_identity(nc, ident[:])
        make_identity(nc, identb[:])

        load_w(0)
        load_bias()
        load_x(0, 0)
        load_x(1, 0)
        load_x(0, 1)
        load_x(1, 1)
        load_w(1)
        load_w(2)

        w_transposes(0, 0)
        w_transposes(0, 1)
        bias_matmul()
        pe_interleave(0, 1)
        w_copy(0, 0)
        x_interleave(0, 0)
        w_quant(0, 0)
        x_quant(0, 0)
        w_copy(0, 1)
        bias_copy()
        x_copy(0, 1)
        pe_interleave(1, 1)
        x_interleave(1, 0)
        w_quant(0, 1)
        x_quant(1, 0)
        x_copy(1, 1)
        x_interleave(0, 2)
        x_quant(0, 1)
        mm(0, 0)
        pe_interleave(0, 3)
        x_copy(0, 3)
        x_quant(0, 2)
        x_quant(1, 1)
        mm(0, 1)
        x_interleave(1, 2)
        pe_interleave(1, 3)

        add_bias(0, 0)
        x_quant(1, 2)
        sumsq(0, 0)
        add_bias(0, 1)
        x_copy(1, 3)
        sumsq(0, 1)
        x_quant(0, 3)
        absmax(0, 0, 0, 2)
        absmax(0, 0, 2, 2)
        x_quant(1, 3)
        w_transposes(1, 0)
        w_transposes(1, 1)
        mm(0, 2)
        mm(0, 3)
        floor_sumsq(0, 0, 0, 4)
        w_copy(1, 0)
        w_copy(1, 1)
        add_bias(0, 2)
        sumsq(0, 2)
        rsqrt_stats(0, 0, 0, 4)
        w_quant(1, 0)
        w_transposes(2, 0)
        w_transposes(2, 1)
        w_copy(2, 0)
        cast_factor(0, 0, 0, 4)
        w_copy(2, 1)
        add_bias(0, 3)
        sumsq(0, 3)
        w_quant(1, 1)
        scale_unit_gpsimd(0, 0)
        cast_unit_scalar(0, 0)
        absmax(0, 1, 0, 2)
        absmax(0, 1, 2, 2)
        w_quant(2, 0)
        w_quant(2, 1)
        mm(1, 0)
        mm(1, 1)
        add_bias(1, 0)
        floor_sumsq(0, 1, 0, 4)
        scale_unit_vector(0, 1)
        cast_unit_scalar(0, 1)
        store_bytes(0, 0)
        sumsq(1, 0)
        rsqrt_stats(0, 1, 0, 4)

        pairs = [(k, c) for k in range(HEADS) for c in range(2)]
        for i in range(2, 5):
            k, c = pairs[i]
            kp, cp = pairs[i - 1]
            kn, cn = pairs[i + 1]
            add_bias(k, 2 * c + 1)
            sumsq_row(k, 2 * c + 1, 0)
            cast_factor(kp, cp, 0, 4)
            sumsq_row(k, 2 * c + 1, 1)
            scale_unit_gpsimd(kp, 2 * cp)
            cast_unit_scalar(kp, 2 * cp)
            cast_unit_scalar(kp, 2 * cp + 1)
            store_bytes(kp, cp)
            absmax(k, c, 0, 2)
            absmax(k, c, 2, 2)
            mm(kn, 2 * cn)
            mm(kn, 2 * cn + 1)
            add_bias(kn, 2 * cn)
            sumsq(kn, 2 * cn)
            floor_sumsq(k, c, 0, 4)
            scale_unit_gpsimd(kp, 2 * cp + 1)
            rsqrt_stats(k, c, 0, 4)

        add_bias(2, 3)
        sumsq_row(2, 3, 0)
        cast_factor(2, 0, 0, 4)
        sumsq_row(2, 3, 1)
        absmax(2, 1, 0, 2)
        scale_unit_vector(2, 0)
        cast_unit_scalar(2, 0)
        floor_sumsq(2, 1, 0, 2)
        absmax(2, 1, 2, 2)
        rsqrt_stats(2, 1, 0, 2)
        cast_factor(2, 1, 0, 2)
        scale_unit_vector(2, 1)
        floor_sumsq(2, 1, 2, 2)
        cast_row_vector(2, 1, 0)
        cast_row_vector(2, 1, 1)
        store_bytes(2, 0)
        rsqrt_stats(2, 1, 2, 2)
        cast_factor(2, 1, 2, 2)
        scale_unit_vector(2, 2)
        cast_row_scalar(2, 2, 0)
        cast_row_vector(2, 2, 1)
        scale_unit_vector(2, 3)
        cast_row_scalar(2, 3, 0)
        cast_row_vector(2, 3, 1)
        store_bytes(2, 1)
